import numpy as np
import ml_dtypes


def mxq(x, axis, fmt="e4m3"):
    dtype, down = {"e4m3": (ml_dtypes.float8_e4m3fn, 7), "e5m2": (ml_dtypes.float8_e5m2, 14)}[fmt]
    v = np.moveaxis(np.asarray(x, np.float32).astype(ml_dtypes.bfloat16).astype(np.float64), axis, -1)
    blocks = v.reshape(v.shape[:-1] + (-1, 32))
    amax = np.abs(blocks).max(-1, keepdims=True)
    byte = np.maximum(np.where(amax > 0, np.frexp(amax)[1] - 1 + 127, 0) - down, 1)
    scale = np.exp2(byte - 127.0)
    codes = (blocks / scale).astype(np.float32).astype(dtype).astype(np.float64)
    return np.moveaxis((codes * scale).reshape(v.shape), -1, axis)


WIDE = False


def mx_kscale(k):
    if not WIDE:
        return np.ones(k)
    levels = np.array([10, -10, 5, -5, 0])
    if k % 512:
        return np.exp2(np.random.permutation(np.resize(levels, k // 32))).repeat(32)
    a = np.empty((k // 512, 16))
    for p in range(k // 512):
        a[p, :8] = np.random.permutation(np.resize(levels, 8))
        for g in range(8):
            far = levels[np.abs(levels - a[p, g]) >= 10]
            a[p, g + 8] = far[np.random.randint(len(far))]
    return np.exp2(a.ravel()).repeat(32)


BF16 = ml_dtypes.bfloat16


def bf(x):
    return np.asarray(x, np.float32).astype(BF16)


def f64(x):
    return np.asarray(x).astype(np.float64)


B, S, D, H, QL, KVL, RD, ND, VD = 2, 2048, 1024, 4, 1536, 512, 128, 64, 64
ROPE_THETA, ROPE_RATIO = 10000.0, 1.0


def rope_tables(seq_len):
    half = RD // 2
    inv_freq = ROPE_RATIO / (ROPE_THETA ** (np.arange(half) * 2.0 / RD))
    freqs = np.arange(seq_len)[:, None] * inv_freq[None, :]
    return np.cos(freqs), np.sin(freqs)


def apply_rope(x, cos, sin):
    x_even = x[..., 0::2]
    x_odd = x[..., 1::2]
    r_even = x_even * cos - x_odd * sin
    r_odd = x_odd * cos + x_even * sin
    return np.stack([r_even, r_odd], axis=-1).reshape(x.shape)


def setup_inputs():
    s, t = mx_kscale(D), mx_kscale(KVL)
    tc = np.concatenate([t, np.ones(RD)])
    return {"hidden_states": bf(np.random.standard_normal((B, S, D)) * s),
            "Wkva": bf(np.random.standard_normal((D, KVL + RD)) / np.sqrt(D) / s[:, None] * tc),
            "Wkvb": bf(np.random.standard_normal((KVL, H * (ND + VD))) / np.sqrt(KVL) / t[:, None])}


def reference(hidden_states, Wkva, Wkvb):
    kv_comp = mxq(f64(hidden_states), 2, "e4m3") @ mxq(f64(Wkva), 0, "e4m3")
    c_kv, k_pe = kv_comp[..., :KVL], kv_comp[..., KVL:]
    cos, sin = rope_tables(S)
    k_pe = apply_rope(k_pe, cos, sin)
    kv = (mxq(c_kv, 2, "e4m3") @ mxq(f64(Wkvb), 0, "e4m3")).reshape(B, S, H, ND + VD)
    kv = kv.transpose(0, 2, 1, 3)
    k_nope, v = kv[..., :ND], kv[..., ND:]
    k_pe_b = np.broadcast_to(k_pe[:, None], (B, H, S, RD))
    k_full = np.concatenate([k_nope, k_pe_b], axis=-1)
    return k_full, v

@@ -1,0 +1,401 @@
+import math
+from contextlib import ExitStack
+
+import concourse.mybir as mybir
+from concourse.masks import make_identity
+
+F32 = mybir.dt.float32
+BF16 = mybir.dt.bfloat16
+I32 = mybir.dt.int32
+U32 = mybir.dt.uint32
+U8 = mybir.dt.uint8
+FP8X4 = mybir.dt.float8_e4m3fn_x4
+ALU = mybir.AluOpType
+ACT = mybir.ActivationFunctionType
+
+P = 128
+PACK = 4
+
+BATCH, SEQ, D_MODEL = 2, 2048, 1024
+HEADS, LATENT, ROPE_DIM, NOPE_DIM, V_DIM = 4, 512, 128, 64, 64
+ROPE_THETA = 10000.0
+ROPE_PAIRS = ROPE_DIM // 2
+
+PASSES = D_MODEL // (P * PACK)
+LATENT_TILES = LATENT // P
+
+SLOTS = 4
+GROUP = P * SLOTS
+GROUPS = BATCH * SEQ // GROUP
+GROUPS_PER_BATCH = SEQ // GROUP
+
+STEP_SLOTS = 2
+STEP_TOKENS = STEP_SLOTS * P
+STEPS_PER_GROUP = SLOTS // STEP_SLOTS
+STEPS = GROUPS * STEPS_PER_GROUP
+
+TAPER_GROUPS = 4
+
+ROUND_MAGIC = 12582912.0
+RUN = 4
+
+FLOPS = 2 * BATCH * SEQ * (D_MODEL * (LATENT + ROPE_DIM) + LATENT * HEADS * (NOPE_DIM + V_DIM))
+
+
+def tile_mlaattention_pb_t_kernel(tc, hidden_states, Wkva, Wkvb, out_0, out_1):
+    nc = tc.nc
+    with ExitStack() as ctx:
+        ctx.enter_context(tc.manual_schedule())
+        const = ctx.enter_context(tc.tile_pool(name="const", bufs=1))
+        x_pool = ctx.enter_context(tc.tile_pool(name="x_pool", bufs=GROUPS))
+        stage = ctx.enter_context(tc.tile_pool(name="stage", bufs=3))
+        out_pool = ctx.enter_context(tc.tile_pool(name="out_pool", bufs=3))
+        psum_xt = ctx.enter_context(tc.psum_pool(name="psum_xt", bufs=2))
+        psum_c = ctx.enter_context(tc.psum_pool(name="psum_c", bufs=2))
+        psum_rope = ctx.enter_context(tc.psum_pool(name="psum_rope", bufs=1))
+        psum_kv = ctx.enter_context(tc.psum_pool(name="psum_kv", bufs=3))
+
+        x_groups = hidden_states.flatten_outer_dims().rearrange("(g p t) d -> g p t d", p=P, t=SLOTS)
+
+        def group_rows(out, group):
+            batch, part = divmod(group, GROUPS_PER_BATCH)
+            rows = out[batch, :, part * GROUP : (part + 1) * GROUP, :]
+            return rows.rearrange("h (p t) d -> p h t d", t=SLOTS)
+
+        wa_raw = const.tile([P, PASSES, PACK, LATENT + ROPE_DIM], BF16)
+        wa_rows = Wkva.rearrange("(c q j) n -> c q j n", c=PASSES, j=PACK)
+        for c in range(PASSES):
+            nc.sync.dma_start(out=wa_raw[:, c], in_=wa_rows[c])
+        wb_raw = const.tile([P, PACK, LATENT], BF16)
+        x_tiles = []
+        for g in range(GROUPS):
+            x_sb = x_pool.tile([P, SLOTS, D_MODEL], BF16)
+            x_tiles.append(x_sb)
+            if g == 0:
+                for first in range(0, SLOTS, STEP_SLOTS):
+                    nc.sync.dma_start(
+                        out=x_sb[:, first : first + STEP_SLOTS, :], in_=x_groups[g][:, first : first + STEP_SLOTS, :]
+                    )
+                nc.sync.dma_start(out=wb_raw[:], in_=Wkvb.rearrange("(q j) n -> q j n", j=PACK))
+            else:
+                nc.sync.dma_start(out=x_sb[:], in_=x_groups[g])
+
+        position_int = const.tile([P, GROUPS_PER_BATCH * SLOTS], I32)
+        nc.gpsimd.iota(
+            position_int[:], pattern=[[GROUP, GROUPS_PER_BATCH], [1, SLOTS]], base=0, channel_multiplier=SLOTS
+        )
+        ident = const.tile([P, P], F32)
+        make_identity(nc, ident[:])
+
+        cos_tab = const.tile([P, GROUPS_PER_BATCH * SLOTS, ROPE_PAIRS], F32)
+        sin_tab = const.tile([P, GROUPS_PER_BATCH * SLOTS, 2, ROPE_PAIRS], F32)
+
+        ones = const.tile([P, 8], F32)
+        nc.vector.memset(ones[:], 1.0)
+        warm = const.tile([P, 8], F32)
+        nc.scalar.activation(out=warm[:], in_=ones[:], func=ACT.Sin)
+
+        coarse = const.tile([P, 8], F32)
+        fine = const.tile([P, 8], F32)
+        for a in range(8):
+            nc.vector.tensor_scalar(
+                out=coarse[:, a : a + 1], in0=ones[:, a : a + 1],
+                scalar1=ROPE_THETA ** (-2.0 * 8 * a / ROPE_DIM) / (2.0 * math.pi), scalar2=None, op0=ALU.mult,
+            )
+            nc.vector.tensor_scalar(
+                out=fine[:, a : a + 1], in0=ones[:, a : a + 1],
+                scalar1=ROPE_THETA ** (-2.0 * a / ROPE_DIM), scalar2=None, op0=ALU.mult,
+            )
+        turns_per_position = const.tile([P, 8, 8], F32)
+        nc.vector.tensor_tensor(
+            out=turns_per_position[:],
+            in0=coarse[:].unsqueeze(2).to_broadcast([P, 8, 8]),
+            in1=fine[:].unsqueeze(1).to_broadcast([P, 8, 8]),
+            op=ALU.mult,
+        )
+
+        position = const.tile([P, GROUPS_PER_BATCH * SLOTS], F32)
+        nc.vector.tensor_copy(out=position[:], in_=position_int[:])
+        half_pi = const.tile([P, 1], F32)
+        nc.vector.tensor_scalar(out=half_pi[:], in0=ones[:, 0:1], scalar1=math.pi / 2.0, scalar2=None, op0=ALU.mult)
+
+        HALVES = 2
+        half_rows = GROUPS_PER_BATCH * SLOTS // HALVES
+        half_shape = [P, half_rows, ROPE_PAIRS]
+        halves = range(HALVES)
+        turns = [const.tile(half_shape, F32, name="turns%d" % h) for h in halves]
+        whole = [const.tile(half_shape, F32, name="whole%d" % h) for h in halves]
+        fraction = [const.tile(half_shape, F32, name="fraction%d" % h) for h in halves]
+        magnitude = [const.tile(half_shape, F32, name="magnitude%d" % h) for h in halves]
+        for h in halves:
+            nc.vector.tensor_tensor(
+                out=turns[h][:],
+                in0=position[:, h * half_rows : (h + 1) * half_rows].unsqueeze(2).to_broadcast(half_shape),
+                in1=turns_per_position[:].rearrange("p a b -> p (a b)").unsqueeze(1).to_broadcast(half_shape),
+                op=ALU.mult,
+            )
+        for h in halves:
+            nc.vector.tensor_scalar(
+                out=whole[h][:], in0=turns[h][:],
+                scalar1=ROUND_MAGIC, scalar2=ROUND_MAGIC, op0=ALU.add, op1=ALU.subtract,
+            )
+        for h in halves:
+            nc.vector.tensor_tensor(out=fraction[h][:], in0=turns[h][:], in1=whole[h][:], op=ALU.subtract)
+
+        for h in halves:
+            nc.scalar.activation(out=magnitude[h][:], in_=fraction[h][:], func=ACT.Abs)
+        wr_grouped = const.tile([P, PASSES, ROPE_DIM, PACK], BF16, align_bytes=64)
+        for c in range(PASSES):
+            nc.scalar.copy(
+                out=wr_grouped[:, c].rearrange("p (m i) j -> p m j i", i=RUN),
+                in_=wa_raw[:, c, :, LATENT:].rearrange("p j (m i) -> p m j i", i=RUN),
+            )
+
+        def sine_pass(number):
+            h, kind = divmod(number, 3)
+            rows = slice(h * half_rows, (h + 1) * half_rows)
+            if kind == 0:
+                nc.scalar.activation(
+                    out=cos_tab[:, rows, :], in_=magnitude[h][:], func=ACT.Sin,
+                    bias=half_pi[:, 0:1], scale=-2.0 * math.pi,
+                )
+            else:
+                sign = (-1.0, 1.0)[kind - 1]
+                nc.scalar.activation(
+                    out=sin_tab[:, rows, kind - 1, :], in_=fraction[h][:], func=ACT.Sin, scale=sign * 2.0 * math.pi
+                )
+
+        wl_grouped = const.tile([P, PASSES, LATENT, PACK], BF16, align_bytes=64)
+        wb_grouped = const.tile([P, 2, HEADS, NOPE_DIM, PACK], BF16, align_bytes=64)
+        wl_codes = const.tile([P, PASSES, LATENT], U32, align_bytes=64)
+        wl_scales = const.tile([P, PASSES, LATENT], U8, align_bytes=64)
+        wr_codes = const.tile([P, PASSES, ROPE_DIM], U32, align_bytes=64)
+        wr_scales = const.tile([P, PASSES, ROPE_DIM], U8, align_bytes=64)
+        wb_codes = const.tile([P, LATENT], U32, align_bytes=64)
+        wb_scales = const.tile([P, LATENT], U8, align_bytes=64)
+
+        for c in range(PASSES):
+            nc.vector.tensor_copy(
+                out=wl_grouped[:, c].rearrange("p (t m) j -> p t m j", t=LATENT_TILES),
+                in_=wa_raw[:, c, :, 0:LATENT].rearrange("p j (m t) -> p t m j", t=LATENT_TILES),
+            )
+        for c in range(PASSES):
+            nc.vector.quantize_mx(
+                out=wl_codes[:, c, :].bitcast(FP8X4),
+                scales=wl_scales[:, c, :],
+                in_=wl_grouped[:, c].rearrange("p n j -> p (n j)"),
+            )
+        nc.vector.quantize_mx(
+            out=wr_codes[:].rearrange("p c n -> p (c n)").bitcast(FP8X4),
+            scales=wr_scales[:].rearrange("p c n -> p (c n)"),
+            in_=wr_grouped[:].rearrange("p c n j -> p (c n j)"),
+        )
+
+        def prepare_wkvb():
+            wb_parts = wb_raw[:].rearrange("p j (h two d) -> p two h d j", two=2, d=NOPE_DIM)
+            for part in range(2):
+                nc.vector.tensor_copy(out=wb_grouped[:, part], in_=wb_parts[:, part])
+            nc.vector.quantize_mx(
+                out=wb_codes[:].bitcast(FP8X4),
+                scales=wb_scales[:],
+                in_=wb_grouped[:].rearrange("p two h d j -> p (two h d j)"),
+            )
+
+        live = {}
+
+        def slots_of(step):
+            return step // STEPS_PER_GROUP, (step % STEPS_PER_GROUP) * STEP_SLOTS
+
+        def transpose_x(step):
+            group, first = slots_of(step)
+            x_grouped = stage.tile([P, PASSES, STEP_TOKENS, 2], F32, align_bytes=64)
+            for s in range(STEP_SLOTS):
+                x_words = x_tiles[group][:, first + s, :].bitcast(F32)
+                xt = psum_xt.tile([P, PASSES * 2, P], F32)
+                for c in range(PASSES):
+                    for u in range(2):
+                        words = x_words[:, 2 * P * c + u : 2 * P * (c + 1) : 2]
+                        nc.tensor.transpose(xt[:, 2 * c + u, :], words, ident[:])
+                nc.scalar.copy(
+                    out=x_grouped[:, :, s * P : (s + 1) * P, :],
+                    in_=xt[:].rearrange("q (c u) r -> q c r u", u=2),
+                )
+            live["x_grouped", step] = x_grouped
+
+        def quantise_x(step):
+            x_codes = stage.tile([P, PASSES, STEP_TOKENS], U32, align_bytes=64)
+            x_scales = stage.tile([P, PASSES, STEP_TOKENS], U8, align_bytes=64)
+            nc.vector.quantize_mx(
+                out=x_codes[:].rearrange("p c r -> p (c r)").bitcast(FP8X4),
+                scales=x_scales[:].rearrange("p c r -> p (c r)"),
+                in_=live["x_grouped", step][:].rearrange("p c r u -> p (c r u)").bitcast(BF16),
+            )
+            live["x_codes", step] = (x_codes, x_scales)
+
+        def project(step):
+            x_codes, x_scales = live["x_codes", step]
+            c_grouped = stage.tile([P, STEP_TOKENS, PACK], BF16, align_bytes=64)
+            for s in range(STEP_SLOTS):
+                tokens = slice(s * P, (s + 1) * P)
+                c_ps = psum_c.tile([P, LATENT_TILES, P], F32)
+                for j in range(LATENT_TILES):
+                    for c in range(PASSES):
+                        nc.tensor.matmul_mx(
+                            out=c_ps[:, j, :],
+                            lhsT=wl_codes[:, c, j * P : (j + 1) * P].bitcast(FP8X4),
+                            lhsT_scale=wl_scales[:, c, j * P : (j + 1) * P],
+                            rhs=x_codes[:, c, tokens].bitcast(FP8X4),
+                            rhs_scale=x_scales[:, c, tokens],
+                            start=(c == 0),
+                            stop=(c == PASSES - 1),
+                        )
+                nc.scalar.copy(out=c_grouped[:, tokens, :], in_=c_ps[:].rearrange("q j r -> q r j"))
+            rope_ps = psum_rope.tile([P, STEP_SLOTS, ROPE_DIM], F32)
+            for s in range(STEP_SLOTS):
+                tokens = slice(s * P, (s + 1) * P)
+                for c in range(PASSES):
+                    nc.tensor.matmul_mx(
+                        out=rope_ps[:, s, :],
+                        lhsT=x_codes[:, c, tokens].bitcast(FP8X4),
+                        lhsT_scale=x_scales[:, c, tokens],
+                        rhs=wr_codes[:, c, :].bitcast(FP8X4),
+                        rhs_scale=wr_scales[:, c, :],
+                        start=(c == 0),
+                        stop=(c == PASSES - 1),
+                    )
+            live["c_grouped", step] = c_grouped
+            live["rope_ps", step] = rope_ps
+
+        def quantise_c(step):
+            c_codes = stage.tile([P, STEP_TOKENS], U32, align_bytes=64)
+            c_scales = stage.tile([P, STEP_TOKENS], U8, align_bytes=64)
+            nc.vector.quantize_mx(
+                out=c_codes[:].bitcast(FP8X4),
+                scales=c_scales[:],
+                in_=live["c_grouped", step][:].rearrange("p r j -> p (r j)"),
+            )
+            live["c_codes", step] = (c_codes, c_scales)
+
+        def rotate_products(step):
+            group, first = slots_of(step)
+            if first == 0:
+                k_out = out_pool.tile([P, HEADS, SLOTS, NOPE_DIM + ROPE_DIM], F32)
+                v_out = out_pool.tile([P, HEADS, SLOTS, V_DIM], F32)
+                live["out", group] = (k_out, v_out)
+            k_out, v_out = live["out", group]
+            table = (group % GROUPS_PER_BATCH) * SLOTS + first
+            pair_shape = [P, STEP_SLOTS, ROPE_PAIRS, 2]
+            rope_pairs = live["rope_ps", step][:].rearrange("p s (i e) -> p s i e", e=2)
+            by_cos = stage.tile(pair_shape, F32)
+            by_sin = stage.tile(pair_shape, F32)
+            nc.vector.tensor_tensor(
+                out=by_cos[:],
+                in0=rope_pairs,
+                in1=cos_tab[:, table : table + STEP_SLOTS, :].unsqueeze(3).to_broadcast(pair_shape),
+                op=ALU.mult,
+            )
+            nc.vector.tensor_tensor(
+                out=by_sin[:],
+                in0=rope_pairs[:, :, :, ::-1],
+                in1=sin_tab[:, table : table + STEP_SLOTS, :, :].rearrange("p s e i -> p s i e"),
+                op=ALU.mult,
+            )
+            live["products", step] = (by_cos, by_sin)
+
+        def rope_rows(step):
+            group, first = slots_of(step)
+            k_out, v_out = live["out", group]
+            return k_out[:, :, first : first + STEP_SLOTS, NOPE_DIM:].rearrange("p h s d -> p s h d")
+
+        def rotate_sum(step):
+            by_cos, by_sin = live["products", step]
+            nc.vector.tensor_tensor(
+                out=rope_rows(step)[:, :, 0, :],
+                in0=by_cos[:].rearrange("p s i e -> p s (i e)"),
+                in1=by_sin[:].rearrange("p s i e -> p s (i e)"),
+                op=ALU.add,
+            )
+
+        def repeat_for_heads(step):
+            nc.vector.tensor_copy(
+                out=rope_rows(step)[:, :, 1:HEADS, :],
+                in_=rope_rows(step)[:, :, 0:1, :].to_broadcast([P, STEP_SLOTS, HEADS - 1, ROPE_DIM]),
+            )
+
+        def expand(step):
+            c_codes, c_scales = live["c_codes", step]
+            nope_ps = psum_kv.tile([P, STEP_SLOTS, HEADS * NOPE_DIM], F32, tag="kv")
+            v_ps = psum_kv.tile([P, STEP_SLOTS, HEADS * V_DIM], F32, tag="kv")
+            half = HEADS * NOPE_DIM
+            for s in range(STEP_SLOTS):
+                tokens = slice(s * P, (s + 1) * P)
+                for part, bank in enumerate((nope_ps, v_ps)):
+                    nc.tensor.matmul_mx(
+                        out=bank[:, s, :],
+                        lhsT=c_codes[:, tokens].bitcast(FP8X4),
+                        lhsT_scale=c_scales[:, tokens],
+                        rhs=wb_codes[:, part * half : (part + 1) * half].bitcast(FP8X4),
+                        rhs_scale=wb_scales[:, part * half : (part + 1) * half],
+                        start=True,
+                        stop=True,
+                    )
+            live["kv_ps", step] = (nope_ps, v_ps)
+
+        def store(group, first, count):
+            k_out, v_out = live["out", group]
+            slots = slice(first, first + count)
+            nc.sync.dma_start(out=group_rows(out_1, group)[:, :, slots, :], in_=v_out[:, :, slots, :])
+            nc.sync.dma_start(out=group_rows(out_0, group)[:, :, slots, :], in_=k_out[:, :, slots, :])
+
+        def take_k_nope(step):
+            group, first = slots_of(step)
+            nope_ps, v_ps = live["kv_ps", step]
+            k_out, v_out = live["out", group]
+            nc.vector.tensor_copy(
+                out=k_out[:, :, first : first + STEP_SLOTS, 0:NOPE_DIM].rearrange("p h s d -> p s h d"),
+                in_=nope_ps[:].rearrange("p s (h d) -> p s h d", h=HEADS),
+            )
+
+        def take_v(step):
+            group, first = slots_of(step)
+            nope_ps, v_ps = live["kv_ps", step]
+            k_out, v_out = live["out", group]
+            nc.scalar.copy(
+                out=v_out[:, :, first : first + STEP_SLOTS, :].rearrange("p h s d -> p s h d"),
+                in_=v_ps[:].rearrange("p s (h d) -> p s h d", h=HEADS),
+            )
+
+        def store_step(step):
+            group, first = slots_of(step)
+            if group >= GROUPS - TAPER_GROUPS:
+                store(group, first, STEP_SLOTS)
+            elif first + STEP_SLOTS == SLOTS:
+                store(group, 0, SLOTS)
+
+        for i in range(STEPS + 3):
+            transposing, projecting, expanding, finishing = i, i - 1, i - 2, i - 3
+            if 0 <= expanding < STEPS:
+                rotate_products(expanding)
+                quantise_c(expanding)
+            if 0 <= finishing < STEPS:
+                take_v(finishing)
+            if transposing < STEPS:
+                transpose_x(transposing)
+            for number in range(2 * i, min(2 * i + 2, 3 * HALVES)):
+                sine_pass(number)
+            if 0 <= finishing < STEPS:
+                take_k_nope(finishing)
+            if 0 <= expanding < STEPS:
+                rotate_sum(expanding)
+            if 0 <= projecting < STEPS:
+                project(projecting)
+            if transposing < STEPS:
+                quantise_x(transposing)
+            if 0 <= expanding < STEPS:
+                repeat_for_heads(expanding)
+            if 0 <= finishing < STEPS:
+                store_step(finishing)
+            if i == 1:
+                prepare_wkvb()
+            if 0 <= expanding < STEPS:
+                expand(expanding)

@@ -24,17 +24,14 @@ ROPE_PAIRS = ROPE_DIM // 2
 PASSES = D_MODEL // (P * PACK)
 LATENT_TILES = LATENT // P
 
-SLOTS = 4
-GROUP = P * SLOTS
-GROUPS = BATCH * SEQ // GROUP
-GROUPS_PER_BATCH = SEQ // GROUP
+SLOTS = SEQ // P
 
-STEP_SLOTS = 2
-STEP_TOKENS = STEP_SLOTS * P
-STEPS_PER_GROUP = SLOTS // STEP_SLOTS
-STEPS = GROUPS * STEPS_PER_GROUP
+UNITS = [(seq, first, 2) for seq in range(BATCH) for first in range(0, SLOTS, 2)]
+UNITS[-1:] = [(BATCH - 1, SLOTS - 2, 1), (BATCH - 1, SLOTS - 1, 1)]
+SINGLE_LOADS = 4
+SINGLE_STORES = 7
 
-TAPER_GROUPS = 4
+TABLE_SLOTS = 4
 
 ROUND_MAGIC = 12582912.0
 RUN = 4
@@ -47,48 +44,52 @@ def tile_mlaattention_pb_t_kernel(tc, hidden_states, Wkva, Wkvb, out_0, out_1):
     with ExitStack() as ctx:
         ctx.enter_context(tc.manual_schedule())
         const = ctx.enter_context(tc.tile_pool(name="const", bufs=1))
-        x_pool = ctx.enter_context(tc.tile_pool(name="x_pool", bufs=GROUPS))
+        x_pool = ctx.enter_context(tc.tile_pool(name="x_pool", bufs=8))
         stage = ctx.enter_context(tc.tile_pool(name="stage", bufs=3))
-        out_pool = ctx.enter_context(tc.tile_pool(name="out_pool", bufs=3))
+        table_pool = ctx.enter_context(tc.tile_pool(name="table_pool", bufs=2))
+        codes_pool = ctx.enter_context(tc.tile_pool(name="codes_pool", bufs=3))
+        out_pool = ctx.enter_context(tc.tile_pool(name="out_pool", bufs=4))
         psum_xt = ctx.enter_context(tc.psum_pool(name="psum_xt", bufs=2))
         psum_c = ctx.enter_context(tc.psum_pool(name="psum_c", bufs=2))
         psum_rope = ctx.enter_context(tc.psum_pool(name="psum_rope", bufs=1))
         psum_kv = ctx.enter_context(tc.psum_pool(name="psum_kv", bufs=3))
 
-        x_groups = hidden_states.flatten_outer_dims().rearrange("(g p t) d -> g p t d", p=P, t=SLOTS)
-
-        def group_rows(out, group):
-            batch, part = divmod(group, GROUPS_PER_BATCH)
-            rows = out[batch, :, part * GROUP : (part + 1) * GROUP, :]
-            return rows.rearrange("h (p t) d -> p h t d", t=SLOTS)
+        x_rows = hidden_states.rearrange("b (p t) d -> b p t d", t=SLOTS)
+        k_rows = out_0.rearrange("b h (p t) d -> b p h t d", t=SLOTS)
+        v_rows = out_1.rearrange("b h (p t) d -> b p h t d", t=SLOTS)
 
         wa_raw = const.tile([P, PASSES, PACK, LATENT + ROPE_DIM], BF16)
         wa_rows = Wkva.rearrange("(c q j) n -> c q j n", c=PASSES, j=PACK)
-        for c in range(PASSES):
-            nc.sync.dma_start(out=wa_raw[:, c], in_=wa_rows[c])
         wb_raw = const.tile([P, PACK, LATENT], BF16)
-        x_tiles = []
-        for g in range(GROUPS):
-            x_sb = x_pool.tile([P, SLOTS, D_MODEL], BF16)
-            x_tiles.append(x_sb)
-            if g == 0:
-                for first in range(0, SLOTS, STEP_SLOTS):
-                    nc.sync.dma_start(
-                        out=x_sb[:, first : first + STEP_SLOTS, :], in_=x_groups[g][:, first : first + STEP_SLOTS, :]
-                    )
-                nc.sync.dma_start(out=wb_raw[:], in_=Wkvb.rearrange("(q j) n -> q j n", j=PACK))
-            else:
-                nc.sync.dma_start(out=x_sb[:], in_=x_groups[g])
+        x_tiles = {}
 
-        position_int = const.tile([P, GROUPS_PER_BATCH * SLOTS], I32)
-        nc.gpsimd.iota(
-            position_int[:], pattern=[[GROUP, GROUPS_PER_BATCH], [1, SLOTS]], base=0, channel_multiplier=SLOTS
-        )
+        def load_x(*units):
+            seq, first, count = UNITS[units[0]]
+            total = sum(UNITS[u][2] for u in units)
+            x_sb = x_pool.tile([P, total, D_MODEL], BF16)
+            nc.sync.dma_start(out=x_sb[:], in_=x_rows[seq][:, first : first + total, :])
+            for u in units:
+                start = UNITS[u][1] - first
+                x_tiles[u] = x_sb[:, start : start + UNITS[u][2], :]
+
+        nc.sync.dma_start(out=wa_raw[:, 0], in_=wa_rows[0])
+        load_x(0)
+        nc.sync.dma_start(out=wa_raw[:, 1], in_=wa_rows[1])
+        load_x(1)
+        nc.sync.dma_start(out=wb_raw[:], in_=Wkvb.rearrange("(q j) n -> q j n", j=PACK))
+        for unit in range(2, SINGLE_LOADS):
+            load_x(unit)
+        for unit in range(SINGLE_LOADS, len(UNITS) - 3, 2):
+            load_x(unit, unit + 1)
+        load_x(*range(len(UNITS) - 3, len(UNITS)))
+
+        position_int = const.tile([P, SLOTS], I32)
+        nc.gpsimd.iota(position_int[:], pattern=[[1, SLOTS]], base=0, channel_multiplier=SLOTS)
         ident = const.tile([P, P], F32)
         make_identity(nc, ident[:])
 
-        cos_tab = const.tile([P, GROUPS_PER_BATCH * SLOTS, ROPE_PAIRS], F32)
-        sin_tab = const.tile([P, GROUPS_PER_BATCH * SLOTS, 2, ROPE_PAIRS], F32)
+        cos_tab = const.tile([P, SLOTS, ROPE_PAIRS], F32)
+        sin_tab = const.tile([P, SLOTS, 2, ROPE_PAIRS], F32)
 
         ones = const.tile([P, 8], F32)
         nc.vector.memset(ones[:], 1.0)
@@ -106,6 +107,8 @@ def tile_mlaattention_pb_t_kernel(tc, hidden_states, Wkva, Wkvb, out_0, out_1):
                 out=fine[:, a : a + 1], in0=ones[:, a : a + 1],
                 scalar1=ROPE_THETA ** (-2.0 * a / ROPE_DIM), scalar2=None, op0=ALU.mult,
             )
+        position = const.tile([P, SLOTS], F32)
+        nc.vector.tensor_copy(out=position[:], in_=position_int[:])
         turns_per_position = const.tile([P, 8, 8], F32)
         nc.vector.tensor_tensor(
             out=turns_per_position[:],
@@ -113,59 +116,65 @@ def tile_mlaattention_pb_t_kernel(tc, hidden_states, Wkva, Wkvb, out_0, out_1):
             in1=fine[:].unsqueeze(1).to_broadcast([P, 8, 8]),
             op=ALU.mult,
         )
-
-        position = const.tile([P, GROUPS_PER_BATCH * SLOTS], F32)
-        nc.vector.tensor_copy(out=position[:], in_=position_int[:])
         half_pi = const.tile([P, 1], F32)
         nc.vector.tensor_scalar(out=half_pi[:], in0=ones[:, 0:1], scalar1=math.pi / 2.0, scalar2=None, op0=ALU.mult)
 
-        HALVES = 2
-        half_rows = GROUPS_PER_BATCH * SLOTS // HALVES
-        half_shape = [P, half_rows, ROPE_PAIRS]
-        halves = range(HALVES)
-        turns = [const.tile(half_shape, F32, name="turns%d" % h) for h in halves]
-        whole = [const.tile(half_shape, F32, name="whole%d" % h) for h in halves]
-        fraction = [const.tile(half_shape, F32, name="fraction%d" % h) for h in halves]
-        magnitude = [const.tile(half_shape, F32, name="magnitude%d" % h) for h in halves]
-        for h in halves:
+        table_shape = [P, TABLE_SLOTS, ROPE_PAIRS]
+        tables = {}
+
+        def table_rows(part):
+            return slice(part * TABLE_SLOTS, (part + 1) * TABLE_SLOTS)
+
+        def table_turns(part):
+            turns = table_pool.tile(table_shape, F32)
             nc.vector.tensor_tensor(
-                out=turns[h][:],
-                in0=position[:, h * half_rows : (h + 1) * half_rows].unsqueeze(2).to_broadcast(half_shape),
-                in1=turns_per_position[:].rearrange("p a b -> p (a b)").unsqueeze(1).to_broadcast(half_shape),
+                out=turns[:],
+                in0=position[:, table_rows(part)].unsqueeze(2).to_broadcast(table_shape),
+                in1=turns_per_position[:].rearrange("p a b -> p (a b)").unsqueeze(1).to_broadcast(table_shape),
                 op=ALU.mult,
             )
-        for h in halves:
+            tables["turns", part] = turns
+
+        def table_whole(part):
+            whole = table_pool.tile(table_shape, F32)
             nc.vector.tensor_scalar(
-                out=whole[h][:], in0=turns[h][:],
+                out=whole[:], in0=tables["turns", part][:],
                 scalar1=ROUND_MAGIC, scalar2=ROUND_MAGIC, op0=ALU.add, op1=ALU.subtract,
             )
-        for h in halves:
-            nc.vector.tensor_tensor(out=fraction[h][:], in0=turns[h][:], in1=whole[h][:], op=ALU.subtract)
+            tables["whole", part] = whole
 
-        for h in halves:
-            nc.scalar.activation(out=magnitude[h][:], in_=fraction[h][:], func=ACT.Abs)
-        wr_grouped = const.tile([P, PASSES, ROPE_DIM, PACK], BF16, align_bytes=64)
-        for c in range(PASSES):
-            nc.scalar.copy(
-                out=wr_grouped[:, c].rearrange("p (m i) j -> p m j i", i=RUN),
-                in_=wa_raw[:, c, :, LATENT:].rearrange("p j (m i) -> p m j i", i=RUN),
+        def table_fraction(part):
+            fraction = table_pool.tile(table_shape, F32)
+            nc.vector.tensor_tensor(
+                out=fraction[:], in0=tables["turns", part][:], in1=tables["whole", part][:], op=ALU.subtract
             )
+            tables["fraction", part] = fraction
 
-        def sine_pass(number):
-            h, kind = divmod(number, 3)
-            rows = slice(h * half_rows, (h + 1) * half_rows)
-            if kind == 0:
-                nc.scalar.activation(
-                    out=cos_tab[:, rows, :], in_=magnitude[h][:], func=ACT.Sin,
-                    bias=half_pi[:, 0:1], scale=-2.0 * math.pi,
-                )
-            else:
-                sign = (-1.0, 1.0)[kind - 1]
-                nc.scalar.activation(
-                    out=sin_tab[:, rows, kind - 1, :], in_=fraction[h][:], func=ACT.Sin, scale=sign * 2.0 * math.pi
-                )
+        def table_sines(part, kinds):
+            fraction = tables["fraction", part]
+            rows = table_rows(part)
+            for kind in kinds:
+                if kind == "magnitude":
+                    magnitude = table_pool.tile(table_shape, F32)
+                    nc.scalar.activation(out=magnitude[:], in_=fraction[:], func=ACT.Abs)
+                    tables["magnitude", part] = magnitude
+                elif kind == "cos":
+                    nc.scalar.activation(
+                        out=cos_tab[:, rows, :], in_=tables["magnitude", part][:], func=ACT.Sin,
+                        bias=half_pi[:, 0:1], scale=-2.0 * math.pi,
+                    )
+                else:
+                    sign = (-1.0, 1.0)[kind]
+                    nc.scalar.activation(
+                        out=sin_tab[:, rows, kind, :], in_=fraction[:], func=ACT.Sin, scale=sign * 2.0 * math.pi
+                    )
 
-        wl_grouped = const.tile([P, PASSES, LATENT, PACK], BF16, align_bytes=64)
+        for step in (table_turns, table_whole, table_fraction):
+            for part in (0, 1):
+                step(part)
+
+        wl_grouped = const.tile([P, PASSES, LATENT_TILES, P, PACK], BF16, align_bytes=64)
+        wr_grouped = const.tile([P, PASSES, ROPE_DIM, PACK], BF16, align_bytes=64)
         wb_grouped = const.tile([P, 2, HEADS, NOPE_DIM, PACK], BF16, align_bytes=64)
         wl_codes = const.tile([P, PASSES, LATENT], U32, align_bytes=64)
         wl_scales = const.tile([P, PASSES, LATENT], U8, align_bytes=64)
@@ -174,27 +183,40 @@ def tile_mlaattention_pb_t_kernel(tc, hidden_states, Wkva, Wkvb, out_0, out_1):
         wb_codes = const.tile([P, LATENT], U32, align_bytes=64)
         wb_scales = const.tile([P, LATENT], U8, align_bytes=64)
 
-        for c in range(PASSES):
-            nc.vector.tensor_copy(
-                out=wl_grouped[:, c].rearrange("p (t m) j -> p t m j", t=LATENT_TILES),
-                in_=wa_raw[:, c, :, 0:LATENT].rearrange("p j (m t) -> p t m j", t=LATENT_TILES),
-            )
-        for c in range(PASSES):
-            nc.vector.quantize_mx(
-                out=wl_codes[:, c, :].bitcast(FP8X4),
-                scales=wl_scales[:, c, :],
-                in_=wl_grouped[:, c].rearrange("p n j -> p (n j)"),
-            )
-        nc.vector.quantize_mx(
-            out=wr_codes[:].rearrange("p c n -> p (c n)").bitcast(FP8X4),
-            scales=wr_scales[:].rearrange("p c n -> p (c n)"),
-            in_=wr_grouped[:].rearrange("p c n j -> p (c n j)"),
-        )
+        def latent_columns(c, tiles):
+            return wa_raw[:, c, :, 0:LATENT].rearrange("p j (m t) -> p t m j", t=LATENT_TILES)[:, tiles]
 
-        def prepare_wkvb():
+        def group_latent(copy, c, first, count):
+            copy(out=wl_grouped[:, c, first : first + count], in_=latent_columns(c, slice(first, first + count)))
+
+        def group_rope(c):
+            nc.scalar.copy(
+                out=wr_grouped[:, c].rearrange("p (m i) j -> p m j i", i=RUN),
+                in_=wa_raw[:, c, :, LATENT:].rearrange("p j (m i) -> p m j i", i=RUN),
+            )
+
+        def quantise_latent(c, first):
+            tiles = slice(first, first + 2)
+            columns = slice(first * P, (first + 2) * P)
+            nc.vector.quantize_mx(
+                out=wl_codes[:, c, columns].bitcast(FP8X4),
+                scales=wl_scales[:, c, columns],
+                in_=wl_grouped[:, c, tiles].rearrange("p t m j -> p (t m j)"),
+            )
+
+        def quantise_rope():
+            nc.vector.quantize_mx(
+                out=wr_codes[:].rearrange("p c n -> p (c n)").bitcast(FP8X4),
+                scales=wr_scales[:].rearrange("p c n -> p (c n)"),
+                in_=wr_grouped[:].rearrange("p c n j -> p (c n j)"),
+            )
+
+        def group_wkvb():
             wb_parts = wb_raw[:].rearrange("p j (h two d) -> p two h d j", two=2, d=NOPE_DIM)
             for part in range(2):
                 nc.vector.tensor_copy(out=wb_grouped[:, part], in_=wb_parts[:, part])
+
+        def quantise_wkvb():
             nc.vector.quantize_mx(
                 out=wb_codes[:].bitcast(FP8X4),
                 scales=wb_scales[:],
@@ -203,14 +225,11 @@ def tile_mlaattention_pb_t_kernel(tc, hidden_states, Wkva, Wkvb, out_0, out_1):
 
         live = {}
 
-        def slots_of(step):
-            return step // STEPS_PER_GROUP, (step % STEPS_PER_GROUP) * STEP_SLOTS
-
-        def transpose_x(step):
-            group, first = slots_of(step)
-            x_grouped = stage.tile([P, PASSES, STEP_TOKENS, 2], F32, align_bytes=64)
-            for s in range(STEP_SLOTS):
-                x_words = x_tiles[group][:, first + s, :].bitcast(F32)
+        def transpose_x(unit):
+            count = UNITS[unit][2]
+            x_grouped = stage.tile([P, PASSES, count * P, 2], F32, align_bytes=64)
+            for s in range(count):
+                x_words = x_tiles[unit][:, s, :].bitcast(F32)
                 xt = psum_xt.tile([P, PASSES * 2, P], F32)
                 for c in range(PASSES):
                     for u in range(2):
@@ -220,22 +239,24 @@ def tile_mlaattention_pb_t_kernel(tc, hidden_states, Wkva, Wkvb, out_0, out_1):
                     out=x_grouped[:, :, s * P : (s + 1) * P, :],
                     in_=xt[:].rearrange("q (c u) r -> q c r u", u=2),
                 )
-            live["x_grouped", step] = x_grouped
+            live["x_grouped", unit] = x_grouped
 
-        def quantise_x(step):
-            x_codes = stage.tile([P, PASSES, STEP_TOKENS], U32, align_bytes=64)
-            x_scales = stage.tile([P, PASSES, STEP_TOKENS], U8, align_bytes=64)
+        def quantise_x(unit):
+            width = UNITS[unit][2] * P
+            x_codes = codes_pool.tile([P, PASSES, width], U32, align_bytes=64)
+            x_scales = codes_pool.tile([P, PASSES, width], U8, align_bytes=64)
             nc.vector.quantize_mx(
                 out=x_codes[:].rearrange("p c r -> p (c r)").bitcast(FP8X4),
                 scales=x_scales[:].rearrange("p c r -> p (c r)"),
-                in_=live["x_grouped", step][:].rearrange("p c r u -> p (c r u)").bitcast(BF16),
+                in_=live["x_grouped", unit][:].rearrange("p c r u -> p (c r u)").bitcast(BF16),
             )
-            live["x_codes", step] = (x_codes, x_scales)
+            live["x_codes", unit] = (x_codes, x_scales)
 
-        def project(step):
-            x_codes, x_scales = live["x_codes", step]
-            c_grouped = stage.tile([P, STEP_TOKENS, PACK], BF16, align_bytes=64)
-            for s in range(STEP_SLOTS):
+        def project(unit):
+            x_codes, x_scales = live["x_codes", unit]
+            count = UNITS[unit][2]
+            c_grouped = stage.tile([P, count * P, PACK], BF16, align_bytes=64)
+            for s in range(count):
                 tokens = slice(s * P, (s + 1) * P)
                 c_ps = psum_c.tile([P, LATENT_TILES, P], F32)
                 for j in range(LATENT_TILES):
@@ -250,8 +271,13 @@ def tile_mlaattention_pb_t_kernel(tc, hidden_states, Wkva, Wkvb, out_0, out_1):
                             stop=(c == PASSES - 1),
                         )
                 nc.scalar.copy(out=c_grouped[:, tokens, :], in_=c_ps[:].rearrange("q j r -> q r j"))
-            rope_ps = psum_rope.tile([P, STEP_SLOTS, ROPE_DIM], F32)
-            for s in range(STEP_SLOTS):
+            live["c_grouped", unit] = c_grouped
+
+        def project_rope(unit):
+            x_codes, x_scales = live["x_codes", unit]
+            count = UNITS[unit][2]
+            rope_ps = psum_rope.tile([P, count, ROPE_DIM], F32)
+            for s in range(count):
                 tokens = slice(s * P, (s + 1) * P)
                 for c in range(PASSES):
                     nc.tensor.matmul_mx(
@@ -263,73 +289,81 @@ def tile_mlaattention_pb_t_kernel(tc, hidden_states, Wkva, Wkvb, out_0, out_1):
                         start=(c == 0),
                         stop=(c == PASSES - 1),
                     )
-            live["c_grouped", step] = c_grouped
-            live["rope_ps", step] = rope_ps
+            live["rope_ps", unit] = rope_ps
 
-        def quantise_c(step):
-            c_codes = stage.tile([P, STEP_TOKENS], U32, align_bytes=64)
-            c_scales = stage.tile([P, STEP_TOKENS], U8, align_bytes=64)
+        stores = [(u, u + 1) for u in range(0, len(UNITS) - SINGLE_STORES, 2)]
+        stores += [(u,) for u in range(len(UNITS) - SINGLE_STORES, len(UNITS))]
+        store_of = {u: group for group in stores for u in group}
+
+        def quantise_c(unit):
+            width = UNITS[unit][2] * P
+            c_codes = stage.tile([P, width], U32, align_bytes=64)
+            c_scales = stage.tile([P, width], U8, align_bytes=64)
             nc.vector.quantize_mx(
                 out=c_codes[:].bitcast(FP8X4),
                 scales=c_scales[:],
-                in_=live["c_grouped", step][:].rearrange("p r j -> p (r j)"),
+                in_=live["c_grouped", unit][:].rearrange("p r j -> p (r j)"),
             )
-            live["c_codes", step] = (c_codes, c_scales)
+            live["c_codes", unit] = (c_codes, c_scales)
 
-        def rotate_products(step):
-            group, first = slots_of(step)
-            if first == 0:
-                k_out = out_pool.tile([P, HEADS, SLOTS, NOPE_DIM + ROPE_DIM], F32)
-                v_out = out_pool.tile([P, HEADS, SLOTS, V_DIM], F32)
+        def rotate_products(unit):
+            seq, first, count = UNITS[unit]
+            group = store_of[unit]
+            if unit == group[0]:
+                total = sum(UNITS[u][2] for u in group)
+                k_out = out_pool.tile([P, HEADS, total, NOPE_DIM + ROPE_DIM], F32)
+                v_out = out_pool.tile([P, HEADS, total, V_DIM], F32)
                 live["out", group] = (k_out, v_out)
-            k_out, v_out = live["out", group]
-            table = (group % GROUPS_PER_BATCH) * SLOTS + first
-            pair_shape = [P, STEP_SLOTS, ROPE_PAIRS, 2]
-            rope_pairs = live["rope_ps", step][:].rearrange("p s (i e) -> p s i e", e=2)
+            pair_shape = [P, count, ROPE_PAIRS, 2]
+            rope_pairs = live["rope_ps", unit][:].rearrange("p s (i e) -> p s i e", e=2)
             by_cos = stage.tile(pair_shape, F32)
             by_sin = stage.tile(pair_shape, F32)
             nc.vector.tensor_tensor(
                 out=by_cos[:],
                 in0=rope_pairs,
-                in1=cos_tab[:, table : table + STEP_SLOTS, :].unsqueeze(3).to_broadcast(pair_shape),
+                in1=cos_tab[:, first : first + count, :].unsqueeze(3).to_broadcast(pair_shape),
                 op=ALU.mult,
             )
             nc.vector.tensor_tensor(
                 out=by_sin[:],
                 in0=rope_pairs[:, :, :, ::-1],
-                in1=sin_tab[:, table : table + STEP_SLOTS, :, :].rearrange("p s e i -> p s i e"),
+                in1=sin_tab[:, first : first + count, :, :].rearrange("p s e i -> p s i e"),
                 op=ALU.mult,
             )
-            live["products", step] = (by_cos, by_sin)
+            live["products", unit] = (by_cos, by_sin)
 
-        def rope_rows(step):
-            group, first = slots_of(step)
-            k_out, v_out = live["out", group]
-            return k_out[:, :, first : first + STEP_SLOTS, NOPE_DIM:].rearrange("p h s d -> p s h d")
+        def out_rows(unit):
+            k_out, v_out = live["out", store_of[unit]]
+            start = UNITS[unit][1] - UNITS[store_of[unit][0]][1]
+            rows = slice(start, start + UNITS[unit][2])
+            return k_out[:, :, rows, :].rearrange("p h s d -> p s h d"), v_out[:, :, rows, :].rearrange("p h s d -> p s h d")
 
-        def rotate_sum(step):
-            by_cos, by_sin = live["products", step]
+        def rotate_sum(unit):
+            by_cos, by_sin = live["products", unit]
+            k_rows_out, v_rows_out = out_rows(unit)
             nc.vector.tensor_tensor(
-                out=rope_rows(step)[:, :, 0, :],
+                out=k_rows_out[:, :, 0, NOPE_DIM:],
                 in0=by_cos[:].rearrange("p s i e -> p s (i e)"),
                 in1=by_sin[:].rearrange("p s i e -> p s (i e)"),
                 op=ALU.add,
             )
 
-        def repeat_for_heads(step):
+        def repeat_for_heads(unit):
+            k_rows_out, v_rows_out = out_rows(unit)
             nc.vector.tensor_copy(
-                out=rope_rows(step)[:, :, 1:HEADS, :],
-                in_=rope_rows(step)[:, :, 0:1, :].to_broadcast([P, STEP_SLOTS, HEADS - 1, ROPE_DIM]),
+                out=k_rows_out[:, :, 1:HEADS, NOPE_DIM:],
+                in_=k_rows_out[:, :, 0:1, NOPE_DIM:].to_broadcast([P, UNITS[unit][2], HEADS - 1, ROPE_DIM]),
             )
 
-        def expand(step):
-            c_codes, c_scales = live["c_codes", step]
-            nope_ps = psum_kv.tile([P, STEP_SLOTS, HEADS * NOPE_DIM], F32, tag="kv")
-            v_ps = psum_kv.tile([P, STEP_SLOTS, HEADS * V_DIM], F32, tag="kv")
+        def expand(unit):
+            c_codes, c_scales = live["c_codes", unit]
+            count = UNITS[unit][2]
+            nope_ps = psum_kv.tile([P, count, HEADS * NOPE_DIM], F32, tag="kv")
+            v_ps = psum_kv.tile([P, count, HEADS * V_DIM], F32, tag="kv")
             half = HEADS * NOPE_DIM
-            for s in range(STEP_SLOTS):
-                tokens = slice(s * P, (s + 1) * P)
-                for part, bank in enumerate((nope_ps, v_ps)):
+            for part, bank in enumerate((nope_ps, v_ps)):
+                for s in range(count):
+                    tokens = slice(s * P, (s + 1) * P)
                     nc.tensor.matmul_mx(
                         out=bank[:, s, :],
                         lhsT=c_codes[:, tokens].bitcast(FP8X4),
@@ -339,63 +373,75 @@ def tile_mlaattention_pb_t_kernel(tc, hidden_states, Wkva, Wkvb, out_0, out_1):
                         start=True,
                         stop=True,
                     )
-            live["kv_ps", step] = (nope_ps, v_ps)
+            live["kv_ps", unit] = (nope_ps, v_ps)
 
-        def store(group, first, count):
-            k_out, v_out = live["out", group]
-            slots = slice(first, first + count)
-            nc.sync.dma_start(out=group_rows(out_1, group)[:, :, slots, :], in_=v_out[:, :, slots, :])
-            nc.sync.dma_start(out=group_rows(out_0, group)[:, :, slots, :], in_=k_out[:, :, slots, :])
-
-        def take_k_nope(step):
-            group, first = slots_of(step)
-            nope_ps, v_ps = live["kv_ps", step]
-            k_out, v_out = live["out", group]
+        def take_k_nope(unit):
+            nope_ps, v_ps = live["kv_ps", unit]
+            k_rows_out, v_rows_out = out_rows(unit)
             nc.vector.tensor_copy(
-                out=k_out[:, :, first : first + STEP_SLOTS, 0:NOPE_DIM].rearrange("p h s d -> p s h d"),
-                in_=nope_ps[:].rearrange("p s (h d) -> p s h d", h=HEADS),
+                out=k_rows_out[:, :, :, 0:NOPE_DIM], in_=nope_ps[:].rearrange("p s (h d) -> p s h d", h=HEADS)
             )
 
-        def take_v(step):
-            group, first = slots_of(step)
-            nope_ps, v_ps = live["kv_ps", step]
-            k_out, v_out = live["out", group]
-            nc.scalar.copy(
-                out=v_out[:, :, first : first + STEP_SLOTS, :].rearrange("p h s d -> p s h d"),
-                in_=v_ps[:].rearrange("p s (h d) -> p s h d", h=HEADS),
-            )
+        def take_v(unit):
+            nope_ps, v_ps = live["kv_ps", unit]
+            k_rows_out, v_rows_out = out_rows(unit)
+            nc.scalar.copy(out=v_rows_out, in_=v_ps[:].rearrange("p s (h d) -> p s h d", h=HEADS))
 
-        def store_step(step):
-            group, first = slots_of(step)
-            if group >= GROUPS - TAPER_GROUPS:
-                store(group, first, STEP_SLOTS)
-            elif first + STEP_SLOTS == SLOTS:
-                store(group, 0, SLOTS)
+        def store(unit):
+            group = store_of[unit]
+            if unit == group[-1]:
+                k_out, v_out = live["out", group]
+                seq, first, count = UNITS[group[0]]
+                rows = slice(first, first + sum(UNITS[u][2] for u in group))
+                nc.sync.dma_start(out=v_rows[seq][:, :, rows, :], in_=v_out[:])
+                nc.sync.dma_start(out=k_rows[seq][:, :, rows, :], in_=k_out[:])
 
-        for i in range(STEPS + 3):
+        for part in (0, 1):
+            table_sines(part, ("magnitude", 0, 1, "cos"))
+        group_rope(0)
+        group_latent(nc.vector.tensor_copy, 0, 0, 2)
+        group_latent(nc.vector.tensor_copy, 0, 2, 2)
+        quantise_latent(0, 0)
+        quantise_latent(0, 2)
+        count = len(UNITS)
+        for i in range(count + 3):
             transposing, projecting, expanding, finishing = i, i - 1, i - 2, i - 3
-            if 0 <= expanding < STEPS:
+            if 0 <= expanding < count:
                 rotate_products(expanding)
                 quantise_c(expanding)
-            if 0 <= finishing < STEPS:
+            if 0 <= finishing < count:
                 take_v(finishing)
-            if transposing < STEPS:
+            if transposing < count:
                 transpose_x(transposing)
-            for number in range(2 * i, min(2 * i + 2, 3 * HALVES)):
-                sine_pass(number)
-            if 0 <= finishing < STEPS:
+            if i == 0:
+                group_latent(nc.scalar.copy, 1, 3, 1)
+                group_rope(1)
+                group_latent(nc.vector.tensor_copy, 1, 0, 2)
+                group_latent(nc.vector.tensor_copy, 1, 2, 1)
+                quantise_latent(1, 0)
+                quantise_x(0)
+                quantise_latent(1, 2)
+                quantise_rope()
+            if 0 <= finishing < count:
                 take_k_nope(finishing)
-            if 0 <= expanding < STEPS:
+            if 0 <= expanding < count:
                 rotate_sum(expanding)
-            if 0 <= projecting < STEPS:
+            if 0 <= projecting < count:
                 project(projecting)
-            if transposing < STEPS:
+                project_rope(projecting)
+            if 0 < transposing < count:
                 quantise_x(transposing)
-            if 0 <= expanding < STEPS:
+            if i in (1, 2, 3):
+                for part in (2, 3):
+                    (table_turns, table_whole, table_fraction)[i - 1](part)
+            if 4 <= i <= 7:
+                table_sines(2 + (i - 4) // 2, (("magnitude", 0), (1, "cos"))[i % 2])
+            if 0 <= expanding < count:
                 repeat_for_heads(expanding)
-            if 0 <= finishing < STEPS:
-                store_step(finishing)
+            if 0 <= finishing < count:
+                store(finishing)
             if i == 1:
-                prepare_wkvb()
-            if 0 <= expanding < STEPS:
+                group_wkvb()
+                quantise_wkvb()
+            if 0 <= expanding < count:
                 expand(expanding)

@@ -26,12 +26,18 @@ LATENT_TILES = LATENT // P
 
 SLOTS = SEQ // P
 
-UNITS = [(seq, first, 2) for seq in range(BATCH) for first in range(0, SLOTS, 2)]
-UNITS[-1:] = [(BATCH - 1, SLOTS - 2, 1), (BATCH - 1, SLOTS - 1, 1)]
-SINGLE_LOADS = 4
-SINGLE_STORES = 7
-
 TABLE_SLOTS = 4
+TABLE_PARTS = SLOTS // TABLE_SLOTS
+UNITS = [
+    (seq, first, 2)
+    for part in range(TABLE_PARTS)
+    for seq in range(BATCH)
+    for first in range(part * TABLE_SLOTS, (part + 1) * TABLE_SLOTS, 2)
+]
+SINGLE_LOADS = 4
+K_STORES = (2,) * 3 + (1,) * 10
+V_STORES = (2,) * 3 + (1,) * 10
+
 
 ROUND_MAGIC = 12582912.0
 RUN = 4
@@ -48,7 +54,8 @@ def tile_mlaattention_pb_t_kernel(tc, hidden_states, Wkva, Wkvb, out_0, out_1):
         stage = ctx.enter_context(tc.tile_pool(name="stage", bufs=3))
         table_pool = ctx.enter_context(tc.tile_pool(name="table_pool", bufs=2))
         codes_pool = ctx.enter_context(tc.tile_pool(name="codes_pool", bufs=3))
-        out_pool = ctx.enter_context(tc.tile_pool(name="out_pool", bufs=4))
+        k_pool = ctx.enter_context(tc.tile_pool(name="k_pool", bufs=4))
+        v_pool = ctx.enter_context(tc.tile_pool(name="v_pool", bufs=4))
         psum_xt = ctx.enter_context(tc.psum_pool(name="psum_xt", bufs=2))
         psum_c = ctx.enter_context(tc.psum_pool(name="psum_c", bufs=2))
         psum_rope = ctx.enter_context(tc.psum_pool(name="psum_rope", bufs=1))
@@ -79,9 +86,8 @@ def tile_mlaattention_pb_t_kernel(tc, hidden_states, Wkva, Wkvb, out_0, out_1):
         nc.sync.dma_start(out=wb_raw[:], in_=Wkvb.rearrange("(q j) n -> q j n", j=PACK))
         for unit in range(2, SINGLE_LOADS):
             load_x(unit)
-        for unit in range(SINGLE_LOADS, len(UNITS) - 3, 2):
+        for unit in range(SINGLE_LOADS, len(UNITS), 2):
             load_x(unit, unit + 1)
-        load_x(*range(len(UNITS) - 3, len(UNITS)))
 
         position_int = const.tile([P, SLOTS], I32)
         nc.gpsimd.iota(position_int[:], pattern=[[1, SLOTS]], base=0, channel_multiplier=SLOTS)
@@ -170,8 +176,7 @@ def tile_mlaattention_pb_t_kernel(tc, hidden_states, Wkva, Wkvb, out_0, out_1):
                     )
 
         for step in (table_turns, table_whole, table_fraction):
-            for part in (0, 1):
-                step(part)
+            step(0)
 
         wl_grouped = const.tile([P, PASSES, LATENT_TILES, P, PACK], BF16, align_bytes=64)
         wr_grouped = const.tile([P, PASSES, ROPE_DIM, PACK], BF16, align_bytes=64)
@@ -211,10 +216,9 @@ def tile_mlaattention_pb_t_kernel(tc, hidden_states, Wkva, Wkvb, out_0, out_1):
                 in_=wr_grouped[:].rearrange("p c n j -> p (c n j)"),
             )
 
-        def group_wkvb():
+        def group_wkvb(copy, part):
             wb_parts = wb_raw[:].rearrange("p j (h two d) -> p two h d j", two=2, d=NOPE_DIM)
-            for part in range(2):
-                nc.vector.tensor_copy(out=wb_grouped[:, part], in_=wb_parts[:, part])
+            copy(out=wb_grouped[:, part], in_=wb_parts[:, part])
 
         def quantise_wkvb():
             nc.vector.quantize_mx(
@@ -291,9 +295,19 @@ def tile_mlaattention_pb_t_kernel(tc, hidden_states, Wkva, Wkvb, out_0, out_1):
                     )
             live["rope_ps", unit] = rope_ps
 
-        stores = [(u, u + 1) for u in range(0, len(UNITS) - SINGLE_STORES, 2)]
-        stores += [(u,) for u in range(len(UNITS) - SINGLE_STORES, len(UNITS))]
-        store_of = {u: group for group in stores for u in group}
+        def runs_of(counts):
+            runs = {}
+            unit = 0
+            for count in counts:
+                for member in range(unit, unit + count):
+                    runs[member] = range(unit, unit + count)
+                unit += count
+            return runs
+
+        k_runs, v_runs = runs_of(K_STORES), runs_of(V_STORES)
+
+        def slots_of(units):
+            return sum(UNITS[u][2] for u in units)
 
         def quantise_c(unit):
             width = UNITS[unit][2] * P
@@ -308,12 +322,12 @@ def tile_mlaattention_pb_t_kernel(tc, hidden_states, Wkva, Wkvb, out_0, out_1):
 
         def rotate_products(unit):
             seq, first, count = UNITS[unit]
-            group = store_of[unit]
-            if unit == group[0]:
-                total = sum(UNITS[u][2] for u in group)
-                k_out = out_pool.tile([P, HEADS, total, NOPE_DIM + ROPE_DIM], F32)
-                v_out = out_pool.tile([P, HEADS, total, V_DIM], F32)
-                live["out", group] = (k_out, v_out)
+            if unit == k_runs[unit][0]:
+                k_out = k_pool.tile([P, HEADS, slots_of(k_runs[unit]), NOPE_DIM + ROPE_DIM], F32)
+                live["k_out", k_runs[unit]] = k_out
+            if unit == v_runs[unit][0]:
+                v_out = v_pool.tile([P, HEADS, slots_of(v_runs[unit]), V_DIM], F32)
+                live["v_out", v_runs[unit]] = v_out
             pair_shape = [P, count, ROPE_PAIRS, 2]
             rope_pairs = live["rope_ps", unit][:].rearrange("p s (i e) -> p s i e", e=2)
             by_cos = stage.tile(pair_shape, F32)
@@ -332,15 +346,16 @@ def tile_mlaattention_pb_t_kernel(tc, hidden_states, Wkva, Wkvb, out_0, out_1):
             )
             live["products", unit] = (by_cos, by_sin)
 
-        def out_rows(unit):
-            k_out, v_out = live["out", store_of[unit]]
-            start = UNITS[unit][1] - UNITS[store_of[unit][0]][1]
-            rows = slice(start, start + UNITS[unit][2])
-            return k_out[:, :, rows, :].rearrange("p h s d -> p s h d"), v_out[:, :, rows, :].rearrange("p h s d -> p s h d")
+        def rows_in(name, units, unit):
+            start = UNITS[unit][1] - UNITS[units[0]][1]
+            return live[name, units][:, :, start : start + UNITS[unit][2], :].rearrange("p h s d -> p s h d")
+
+        def k_rows_of(unit):
+            return rows_in("k_out", k_runs[unit], unit)
 
         def rotate_sum(unit):
             by_cos, by_sin = live["products", unit]
-            k_rows_out, v_rows_out = out_rows(unit)
+            k_rows_out = k_rows_of(unit)
             nc.vector.tensor_tensor(
                 out=k_rows_out[:, :, 0, NOPE_DIM:],
                 in0=by_cos[:].rearrange("p s i e -> p s (i e)"),
@@ -349,7 +364,7 @@ def tile_mlaattention_pb_t_kernel(tc, hidden_states, Wkva, Wkvb, out_0, out_1):
             )
 
         def repeat_for_heads(unit):
-            k_rows_out, v_rows_out = out_rows(unit)
+            k_rows_out = k_rows_of(unit)
             nc.vector.tensor_copy(
                 out=k_rows_out[:, :, 1:HEADS, NOPE_DIM:],
                 in_=k_rows_out[:, :, 0:1, NOPE_DIM:].to_broadcast([P, UNITS[unit][2], HEADS - 1, ROPE_DIM]),
@@ -377,27 +392,28 @@ def tile_mlaattention_pb_t_kernel(tc, hidden_states, Wkva, Wkvb, out_0, out_1):
 
         def take_k_nope(unit):
             nope_ps, v_ps = live["kv_ps", unit]
-            k_rows_out, v_rows_out = out_rows(unit)
+            k_rows_out = k_rows_of(unit)
             nc.vector.tensor_copy(
                 out=k_rows_out[:, :, :, 0:NOPE_DIM], in_=nope_ps[:].rearrange("p s (h d) -> p s h d", h=HEADS)
             )
 
         def take_v(unit):
             nope_ps, v_ps = live["kv_ps", unit]
-            k_rows_out, v_rows_out = out_rows(unit)
-            nc.scalar.copy(out=v_rows_out, in_=v_ps[:].rearrange("p s (h d) -> p s h d", h=HEADS))
+            nc.scalar.copy(
+                out=rows_in("v_out", v_runs[unit], unit), in_=v_ps[:].rearrange("p s (h d) -> p s h d", h=HEADS)
+            )
+
+        def store_run(name, runs, dram, unit):
+            if unit == runs[unit][-1]:
+                seq, first, count = UNITS[runs[unit][0]]
+                rows = slice(first, first + slots_of(runs[unit]))
+                nc.sync.dma_start(out=dram[seq][:, :, rows, :], in_=live[name, runs[unit]][:])
 
         def store(unit):
-            group = store_of[unit]
-            if unit == group[-1]:
-                k_out, v_out = live["out", group]
-                seq, first, count = UNITS[group[0]]
-                rows = slice(first, first + sum(UNITS[u][2] for u in group))
-                nc.sync.dma_start(out=v_rows[seq][:, :, rows, :], in_=v_out[:])
-                nc.sync.dma_start(out=k_rows[seq][:, :, rows, :], in_=k_out[:])
+            store_run("v_out", v_runs, v_rows, unit)
+            store_run("k_out", k_runs, k_rows, unit)
 
-        for part in (0, 1):
-            table_sines(part, ("magnitude", 0, 1, "cos"))
+        table_sines(0, ("magnitude", 0, 1, "cos"))
         group_rope(0)
         group_latent(nc.vector.tensor_copy, 0, 0, 2)
         group_latent(nc.vector.tensor_copy, 0, 2, 2)
@@ -426,22 +442,25 @@ def tile_mlaattention_pb_t_kernel(tc, hidden_states, Wkva, Wkvb, out_0, out_1):
                 take_k_nope(finishing)
             if 0 <= expanding < count:
                 rotate_sum(expanding)
+            if i == 1:
+                group_wkvb(nc.scalar.copy, 1)
             if 0 <= projecting < count:
                 project(projecting)
                 project_rope(projecting)
             if 0 < transposing < count:
                 quantise_x(transposing)
-            if i in (1, 2, 3):
-                for part in (2, 3):
-                    (table_turns, table_whole, table_fraction)[i - 1](part)
-            if 4 <= i <= 7:
-                table_sines(2 + (i - 4) // 2, (("magnitude", 0), (1, "cos"))[i % 2])
+            part, step = divmod(i + 3, 4)
+            if 0 < part < 4 and step < 3:
+                (table_turns, table_whole, table_fraction)[step](part)
+            part, step = divmod(i + 0, 4)
+            if 0 < part < 4 and step < 2:
+                table_sines(part, (("magnitude", 0), (1, "cos"))[step])
             if 0 <= expanding < count:
                 repeat_for_heads(expanding)
             if 0 <= finishing < count:
                 store(finishing)
             if i == 1:
-                group_wkvb()
+                group_wkvb(nc.vector.tensor_copy, 0)
                 quantise_wkvb()
             if 0 <= expanding < count:
                 expand(expanding)

@@ -35,8 +35,8 @@ UNITS = [
     for first in range(part * TABLE_SLOTS, (part + 1) * TABLE_SLOTS, 2)
 ]
 SINGLE_LOADS = 4
-K_STORES = (2,) * 3 + (1,) * 10
-V_STORES = (2,) * 3 + (1,) * 10
+K_STORES = (2,) * 4 + (1,) * 8
+V_STORES = (2,) * 6 + (1,) * 4
 
 
 ROUND_MAGIC = 12582912.0
@@ -176,7 +176,8 @@ def tile_mlaattention_pb_t_kernel(tc, hidden_states, Wkva, Wkvb, out_0, out_1):
                     )
 
         for step in (table_turns, table_whole, table_fraction):
-            step(0)
+            for part in (0, 1):
+                step(part)
 
         wl_grouped = const.tile([P, PASSES, LATENT_TILES, P, PACK], BF16, align_bytes=64)
         wr_grouped = const.tile([P, PASSES, ROPE_DIM, PACK], BF16, align_bytes=64)
@@ -425,6 +426,9 @@ def tile_mlaattention_pb_t_kernel(tc, hidden_states, Wkva, Wkvb, out_0, out_1):
             if 0 <= expanding < count:
                 rotate_products(expanding)
                 quantise_c(expanding)
+            part, step = divmod(i + 2, 4)
+            if 0 < part < TABLE_PARTS:
+                table_sines(part, (("magnitude", 0, "cos", 1)[step],))
             if 0 <= finishing < count:
                 take_v(finishing)
             if transposing < count:
@@ -449,12 +453,9 @@ def tile_mlaattention_pb_t_kernel(tc, hidden_states, Wkva, Wkvb, out_0, out_1):
                 project_rope(projecting)
             if 0 < transposing < count:
                 quantise_x(transposing)
-            part, step = divmod(i + 3, 4)
-            if 0 < part < 4 and step < 3:
+            part, step = divmod(i + 5, 4)
+            if 1 < part < TABLE_PARTS and step < 3:
                 (table_turns, table_whole, table_fraction)[step](part)
-            part, step = divmod(i + 0, 4)
-            if 0 < part < 4 and step < 2:
-                table_sines(part, (("magnitude", 0), (1, "cos"))[step])
             if 0 <= expanding < count:
                 repeat_for_heads(expanding)
             if 0 <= finishing < count:

import math
from contextlib import ExitStack

import concourse.mybir as mybir
from concourse.masks import make_identity

F32 = mybir.dt.float32
BF16 = mybir.dt.bfloat16
I32 = mybir.dt.int32
U32 = mybir.dt.uint32
U8 = mybir.dt.uint8
FP8X4 = mybir.dt.float8_e4m3fn_x4
ALU = mybir.AluOpType
ACT = mybir.ActivationFunctionType

P = 128
PACK = 4

BATCH, SEQ, D_MODEL = 2, 2048, 1024
HEADS, LATENT, ROPE_DIM, NOPE_DIM, V_DIM = 4, 512, 128, 64, 64
ROPE_THETA = 10000.0
ROPE_PAIRS = ROPE_DIM // 2

PASSES = D_MODEL // (P * PACK)
LATENT_TILES = LATENT // P

SLOTS = SEQ // P

TABLE_SLOTS = 4
TABLE_PARTS = SLOTS // TABLE_SLOTS
UNITS = [
    (seq, first, 2)
    for part in range(TABLE_PARTS)
    for seq in range(BATCH)
    for first in range(part * TABLE_SLOTS, (part + 1) * TABLE_SLOTS, 2)
]
SINGLE_LOADS = 4
K_STORES = (2,) * 4 + (1,) * 8
V_STORES = (2,) * 6 + (1,) * 4


ROUND_MAGIC = 12582912.0
RUN = 4

FLOPS = 2 * BATCH * SEQ * (D_MODEL * (LATENT + ROPE_DIM) + LATENT * HEADS * (NOPE_DIM + V_DIM))


def tile_mlaattention_pb_t_kernel(tc, hidden_states, Wkva, Wkvb, out_0, out_1):
    nc = tc.nc
    with ExitStack() as ctx:
        ctx.enter_context(tc.manual_schedule())
        const = ctx.enter_context(tc.tile_pool(name="const", bufs=1))
        x_pool = ctx.enter_context(tc.tile_pool(name="x_pool", bufs=8))
        stage = ctx.enter_context(tc.tile_pool(name="stage", bufs=3))
        table_pool = ctx.enter_context(tc.tile_pool(name="table_pool", bufs=2))
        codes_pool = ctx.enter_context(tc.tile_pool(name="codes_pool", bufs=3))
        k_pool = ctx.enter_context(tc.tile_pool(name="k_pool", bufs=4))
        v_pool = ctx.enter_context(tc.tile_pool(name="v_pool", bufs=4))
        psum_xt = ctx.enter_context(tc.psum_pool(name="psum_xt", bufs=2))
        psum_c = ctx.enter_context(tc.psum_pool(name="psum_c", bufs=2))
        psum_rope = ctx.enter_context(tc.psum_pool(name="psum_rope", bufs=1))
        psum_kv = ctx.enter_context(tc.psum_pool(name="psum_kv", bufs=3))

        x_rows = hidden_states.rearrange("b (p t) d -> b p t d", t=SLOTS)
        k_rows = out_0.rearrange("b h (p t) d -> b p h t d", t=SLOTS)
        v_rows = out_1.rearrange("b h (p t) d -> b p h t d", t=SLOTS)

        wa_raw = const.tile([P, PASSES, PACK, LATENT + ROPE_DIM], BF16)
        wa_rows = Wkva.rearrange("(c q j) n -> c q j n", c=PASSES, j=PACK)
        wb_raw = const.tile([P, PACK, LATENT], BF16)
        x_tiles = {}

        def load_x(*units):
            seq, first, count = UNITS[units[0]]
            total = sum(UNITS[u][2] for u in units)
            x_sb = x_pool.tile([P, total, D_MODEL], BF16)
            nc.sync.dma_start(out=x_sb[:], in_=x_rows[seq][:, first : first + total, :])
            for u in units:
                start = UNITS[u][1] - first
                x_tiles[u] = x_sb[:, start : start + UNITS[u][2], :]

        nc.sync.dma_start(out=wa_raw[:, 0], in_=wa_rows[0])
        load_x(0)
        nc.sync.dma_start(out=wa_raw[:, 1], in_=wa_rows[1])
        load_x(1)
        nc.sync.dma_start(out=wb_raw[:], in_=Wkvb.rearrange("(q j) n -> q j n", j=PACK))
        for unit in range(2, SINGLE_LOADS):
            load_x(unit)
        for unit in range(SINGLE_LOADS, len(UNITS), 2):
            load_x(unit, unit + 1)

        position_int = const.tile([P, SLOTS], I32)
        nc.gpsimd.iota(position_int[:], pattern=[[1, SLOTS]], base=0, channel_multiplier=SLOTS)
        ident = const.tile([P, P], F32)
        make_identity(nc, ident[:])

        cos_tab = const.tile([P, SLOTS, ROPE_PAIRS], F32)
        sin_tab = const.tile([P, SLOTS, 2, ROPE_PAIRS], F32)

        ones = const.tile([P, 8], F32)
        nc.vector.memset(ones[:], 1.0)
        warm = const.tile([P, 8], F32)
        nc.scalar.activation(out=warm[:], in_=ones[:], func=ACT.Sin)

        coarse = const.tile([P, 8], F32)
        fine = const.tile([P, 8], F32)
        for a in range(8):
            nc.vector.tensor_scalar(
                out=coarse[:, a : a + 1], in0=ones[:, a : a + 1],
                scalar1=ROPE_THETA ** (-2.0 * 8 * a / ROPE_DIM) / (2.0 * math.pi), scalar2=None, op0=ALU.mult,
            )
            nc.vector.tensor_scalar(
                out=fine[:, a : a + 1], in0=ones[:, a : a + 1],
                scalar1=ROPE_THETA ** (-2.0 * a / ROPE_DIM), scalar2=None, op0=ALU.mult,
            )
        position = const.tile([P, SLOTS], F32)
        nc.vector.tensor_copy(out=position[:], in_=position_int[:])
        turns_per_position = const.tile([P, 8, 8], F32)
        nc.vector.tensor_tensor(
            out=turns_per_position[:],
            in0=coarse[:].unsqueeze(2).to_broadcast([P, 8, 8]),
            in1=fine[:].unsqueeze(1).to_broadcast([P, 8, 8]),
            op=ALU.mult,
        )
        half_pi = const.tile([P, 1], F32)
        nc.vector.tensor_scalar(out=half_pi[:], in0=ones[:, 0:1], scalar1=math.pi / 2.0, scalar2=None, op0=ALU.mult)

        table_shape = [P, TABLE_SLOTS, ROPE_PAIRS]
        tables = {}

        def table_rows(part):
            return slice(part * TABLE_SLOTS, (part + 1) * TABLE_SLOTS)

        def table_turns(part):
            turns = table_pool.tile(table_shape, F32)
            nc.vector.tensor_tensor(
                out=turns[:],
                in0=position[:, table_rows(part)].unsqueeze(2).to_broadcast(table_shape),
                in1=turns_per_position[:].rearrange("p a b -> p (a b)").unsqueeze(1).to_broadcast(table_shape),
                op=ALU.mult,
            )
            tables["turns", part] = turns

        def table_whole(part):
            whole = table_pool.tile(table_shape, F32)
            nc.vector.tensor_scalar(
                out=whole[:], in0=tables["turns", part][:],
                scalar1=ROUND_MAGIC, scalar2=ROUND_MAGIC, op0=ALU.add, op1=ALU.subtract,
            )
            tables["whole", part] = whole

        def table_fraction(part):
            fraction = table_pool.tile(table_shape, F32)
            nc.vector.tensor_tensor(
                out=fraction[:], in0=tables["turns", part][:], in1=tables["whole", part][:], op=ALU.subtract
            )
            tables["fraction", part] = fraction

        def table_sines(part, kinds):
            fraction = tables["fraction", part]
            rows = table_rows(part)
            for kind in kinds:
                if kind == "magnitude":
                    magnitude = table_pool.tile(table_shape, F32)
                    nc.scalar.activation(out=magnitude[:], in_=fraction[:], func=ACT.Abs)
                    tables["magnitude", part] = magnitude
                elif kind == "cos":
                    nc.scalar.activation(
                        out=cos_tab[:, rows, :], in_=tables["magnitude", part][:], func=ACT.Sin,
                        bias=half_pi[:, 0:1], scale=-2.0 * math.pi,
                    )
                else:
                    sign = (-1.0, 1.0)[kind]
                    nc.scalar.activation(
                        out=sin_tab[:, rows, kind, :], in_=fraction[:], func=ACT.Sin, scale=sign * 2.0 * math.pi
                    )

        for step in (table_turns, table_whole, table_fraction):
            for part in (0, 1):
                step(part)

        wl_grouped = const.tile([P, PASSES, LATENT_TILES, P, PACK], BF16, align_bytes=64)
        wr_grouped = const.tile([P, PASSES, ROPE_DIM, PACK], BF16, align_bytes=64)
        wb_grouped = const.tile([P, 2, HEADS, NOPE_DIM, PACK], BF16, align_bytes=64)
        wl_codes = const.tile([P, PASSES, LATENT], U32, align_bytes=64)
        wl_scales = const.tile([P, PASSES, LATENT], U8, align_bytes=64)
        wr_codes = const.tile([P, PASSES, ROPE_DIM], U32, align_bytes=64)
        wr_scales = const.tile([P, PASSES, ROPE_DIM], U8, align_bytes=64)
        wb_codes = const.tile([P, LATENT], U32, align_bytes=64)
        wb_scales = const.tile([P, LATENT], U8, align_bytes=64)

        def latent_columns(c, tiles):
            return wa_raw[:, c, :, 0:LATENT].rearrange("p j (m t) -> p t m j", t=LATENT_TILES)[:, tiles]

        def group_latent(copy, c, first, count):
            copy(out=wl_grouped[:, c, first : first + count], in_=latent_columns(c, slice(first, first + count)))

        def group_rope(c):
            nc.scalar.copy(
                out=wr_grouped[:, c].rearrange("p (m i) j -> p m j i", i=RUN),
                in_=wa_raw[:, c, :, LATENT:].rearrange("p j (m i) -> p m j i", i=RUN),
            )

        def quantise_latent(c, first):
            tiles = slice(first, first + 2)
            columns = slice(first * P, (first + 2) * P)
            nc.vector.quantize_mx(
                out=wl_codes[:, c, columns].bitcast(FP8X4),
                scales=wl_scales[:, c, columns],
                in_=wl_grouped[:, c, tiles].rearrange("p t m j -> p (t m j)"),
            )

        def quantise_rope():
            nc.vector.quantize_mx(
                out=wr_codes[:].rearrange("p c n -> p (c n)").bitcast(FP8X4),
                scales=wr_scales[:].rearrange("p c n -> p (c n)"),
                in_=wr_grouped[:].rearrange("p c n j -> p (c n j)"),
            )

        def group_wkvb(copy, part):
            wb_parts = wb_raw[:].rearrange("p j (h two d) -> p two h d j", two=2, d=NOPE_DIM)
            copy(out=wb_grouped[:, part], in_=wb_parts[:, part])

        def quantise_wkvb():
            nc.vector.quantize_mx(
                out=wb_codes[:].bitcast(FP8X4),
                scales=wb_scales[:],
                in_=wb_grouped[:].rearrange("p two h d j -> p (two h d j)"),
            )

        live = {}

        def transpose_x(unit):
            count = UNITS[unit][2]
            x_grouped = stage.tile([P, PASSES, count * P, 2], F32, align_bytes=64)
            for s in range(count):
                x_words = x_tiles[unit][:, s, :].bitcast(F32)
                xt = psum_xt.tile([P, PASSES * 2, P], F32)
                for c in range(PASSES):
                    for u in range(2):
                        words = x_words[:, 2 * P * c + u : 2 * P * (c + 1) : 2]
                        nc.tensor.transpose(xt[:, 2 * c + u, :], words, ident[:])
                nc.scalar.copy(
                    out=x_grouped[:, :, s * P : (s + 1) * P, :],
                    in_=xt[:].rearrange("q (c u) r -> q c r u", u=2),
                )
            live["x_grouped", unit] = x_grouped

        def quantise_x(unit):
            width = UNITS[unit][2] * P
            x_codes = codes_pool.tile([P, PASSES, width], U32, align_bytes=64)
            x_scales = codes_pool.tile([P, PASSES, width], U8, align_bytes=64)
            nc.vector.quantize_mx(
                out=x_codes[:].rearrange("p c r -> p (c r)").bitcast(FP8X4),
                scales=x_scales[:].rearrange("p c r -> p (c r)"),
                in_=live["x_grouped", unit][:].rearrange("p c r u -> p (c r u)").bitcast(BF16),
            )
            live["x_codes", unit] = (x_codes, x_scales)

        def project(unit):
            x_codes, x_scales = live["x_codes", unit]
            count = UNITS[unit][2]
            c_grouped = stage.tile([P, count * P, PACK], BF16, align_bytes=64)
            for s in range(count):
                tokens = slice(s * P, (s + 1) * P)
                c_ps = psum_c.tile([P, LATENT_TILES, P], F32)
                for j in range(LATENT_TILES):
                    for c in range(PASSES):
                        nc.tensor.matmul_mx(
                            out=c_ps[:, j, :],
                            lhsT=wl_codes[:, c, j * P : (j + 1) * P].bitcast(FP8X4),
                            lhsT_scale=wl_scales[:, c, j * P : (j + 1) * P],
                            rhs=x_codes[:, c, tokens].bitcast(FP8X4),
                            rhs_scale=x_scales[:, c, tokens],
                            start=(c == 0),
                            stop=(c == PASSES - 1),
                        )
                nc.scalar.copy(out=c_grouped[:, tokens, :], in_=c_ps[:].rearrange("q j r -> q r j"))
            live["c_grouped", unit] = c_grouped

        def project_rope(unit):
            x_codes, x_scales = live["x_codes", unit]
            count = UNITS[unit][2]
            rope_ps = psum_rope.tile([P, count, ROPE_DIM], F32)
            for s in range(count):
                tokens = slice(s * P, (s + 1) * P)
                for c in range(PASSES):
                    nc.tensor.matmul_mx(
                        out=rope_ps[:, s, :],
                        lhsT=x_codes[:, c, tokens].bitcast(FP8X4),
                        lhsT_scale=x_scales[:, c, tokens],
                        rhs=wr_codes[:, c, :].bitcast(FP8X4),
                        rhs_scale=wr_scales[:, c, :],
                        start=(c == 0),
                        stop=(c == PASSES - 1),
                    )
            live["rope_ps", unit] = rope_ps

        def runs_of(counts):
            runs = {}
            unit = 0
            for count in counts:
                for member in range(unit, unit + count):
                    runs[member] = range(unit, unit + count)
                unit += count
            return runs

        k_runs, v_runs = runs_of(K_STORES), runs_of(V_STORES)

        def slots_of(units):
            return sum(UNITS[u][2] for u in units)

        def quantise_c(unit):
            width = UNITS[unit][2] * P
            c_codes = stage.tile([P, width], U32, align_bytes=64)
            c_scales = stage.tile([P, width], U8, align_bytes=64)
            nc.vector.quantize_mx(
                out=c_codes[:].bitcast(FP8X4),
                scales=c_scales[:],
                in_=live["c_grouped", unit][:].rearrange("p r j -> p (r j)"),
            )
            live["c_codes", unit] = (c_codes, c_scales)

        def rotate_products(unit):
            seq, first, count = UNITS[unit]
            if unit == k_runs[unit][0]:
                k_out = k_pool.tile([P, HEADS, slots_of(k_runs[unit]), NOPE_DIM + ROPE_DIM], F32)
                live["k_out", k_runs[unit]] = k_out
            if unit == v_runs[unit][0]:
                v_out = v_pool.tile([P, HEADS, slots_of(v_runs[unit]), V_DIM], F32)
                live["v_out", v_runs[unit]] = v_out
            pair_shape = [P, count, ROPE_PAIRS, 2]
            rope_pairs = live["rope_ps", unit][:].rearrange("p s (i e) -> p s i e", e=2)
            by_cos = stage.tile(pair_shape, F32)
            by_sin = stage.tile(pair_shape, F32)
            nc.vector.tensor_tensor(
                out=by_cos[:],
                in0=rope_pairs,
                in1=cos_tab[:, first : first + count, :].unsqueeze(3).to_broadcast(pair_shape),
                op=ALU.mult,
            )
            nc.vector.tensor_tensor(
                out=by_sin[:],
                in0=rope_pairs[:, :, :, ::-1],
                in1=sin_tab[:, first : first + count, :, :].rearrange("p s e i -> p s i e"),
                op=ALU.mult,
            )
            live["products", unit] = (by_cos, by_sin)

        def rows_in(name, units, unit):
            start = UNITS[unit][1] - UNITS[units[0]][1]
            return live[name, units][:, :, start : start + UNITS[unit][2], :].rearrange("p h s d -> p s h d")

        def k_rows_of(unit):
            return rows_in("k_out", k_runs[unit], unit)

        def rotate_sum(unit):
            by_cos, by_sin = live["products", unit]
            k_rows_out = k_rows_of(unit)
            nc.vector.tensor_tensor(
                out=k_rows_out[:, :, 0, NOPE_DIM:],
                in0=by_cos[:].rearrange("p s i e -> p s (i e)"),
                in1=by_sin[:].rearrange("p s i e -> p s (i e)"),
                op=ALU.add,
            )

        def repeat_for_heads(unit):
            k_rows_out = k_rows_of(unit)
            nc.vector.tensor_copy(
                out=k_rows_out[:, :, 1:HEADS, NOPE_DIM:],
                in_=k_rows_out[:, :, 0:1, NOPE_DIM:].to_broadcast([P, UNITS[unit][2], HEADS - 1, ROPE_DIM]),
            )

        def expand(unit):
            c_codes, c_scales = live["c_codes", unit]
            count = UNITS[unit][2]
            nope_ps = psum_kv.tile([P, count, HEADS * NOPE_DIM], F32, tag="kv")
            v_ps = psum_kv.tile([P, count, HEADS * V_DIM], F32, tag="kv")
            half = HEADS * NOPE_DIM
            for part, bank in enumerate((nope_ps, v_ps)):
                for s in range(count):
                    tokens = slice(s * P, (s + 1) * P)
                    nc.tensor.matmul_mx(
                        out=bank[:, s, :],
                        lhsT=c_codes[:, tokens].bitcast(FP8X4),
                        lhsT_scale=c_scales[:, tokens],
                        rhs=wb_codes[:, part * half : (part + 1) * half].bitcast(FP8X4),
                        rhs_scale=wb_scales[:, part * half : (part + 1) * half],
                        start=True,
                        stop=True,
                    )
            live["kv_ps", unit] = (nope_ps, v_ps)

        def take_k_nope(unit):
            nope_ps, v_ps = live["kv_ps", unit]
            k_rows_out = k_rows_of(unit)
            nc.vector.tensor_copy(
                out=k_rows_out[:, :, :, 0:NOPE_DIM], in_=nope_ps[:].rearrange("p s (h d) -> p s h d", h=HEADS)
            )

        def take_v(unit):
            nope_ps, v_ps = live["kv_ps", unit]
            nc.scalar.copy(
                out=rows_in("v_out", v_runs[unit], unit), in_=v_ps[:].rearrange("p s (h d) -> p s h d", h=HEADS)
            )

        def store_run(name, runs, dram, unit):
            if unit == runs[unit][-1]:
                seq, first, count = UNITS[runs[unit][0]]
                rows = slice(first, first + slots_of(runs[unit]))
                nc.sync.dma_start(out=dram[seq][:, :, rows, :], in_=live[name, runs[unit]][:])

        def store(unit):
            store_run("v_out", v_runs, v_rows, unit)
            store_run("k_out", k_runs, k_rows, unit)

        table_sines(0, ("magnitude", 0, 1, "cos"))
        group_rope(0)
        group_latent(nc.vector.tensor_copy, 0, 0, 2)
        group_latent(nc.vector.tensor_copy, 0, 2, 2)
        quantise_latent(0, 0)
        quantise_latent(0, 2)
        count = len(UNITS)
        for i in range(count + 3):
            transposing, projecting, expanding, finishing = i, i - 1, i - 2, i - 3
            if 0 <= expanding < count:
                rotate_products(expanding)
                quantise_c(expanding)
            part, step = divmod(i + 2, 4)
            if 0 < part < TABLE_PARTS:
                table_sines(part, (("magnitude", 0, "cos", 1)[step],))
            if 0 <= finishing < count:
                take_v(finishing)
            if transposing < count:
                transpose_x(transposing)
            if i == 0:
                group_latent(nc.scalar.copy, 1, 3, 1)
                group_rope(1)
                group_latent(nc.vector.tensor_copy, 1, 0, 2)
                group_latent(nc.vector.tensor_copy, 1, 2, 1)
                quantise_latent(1, 0)
                quantise_x(0)
                quantise_latent(1, 2)
                quantise_rope()
            if 0 <= finishing < count:
                take_k_nope(finishing)
            if 0 <= expanding < count:
                rotate_sum(expanding)
            if i == 1:
                group_wkvb(nc.scalar.copy, 1)
            if 0 <= projecting < count:
                project(projecting)
                project_rope(projecting)
            if 0 < transposing < count:
                quantise_x(transposing)
            part, step = divmod(i + 5, 4)
            if 1 < part < TABLE_PARTS and step < 3:
                (table_turns, table_whole, table_fraction)[step](part)
            if 0 <= expanding < count:
                repeat_for_heads(expanding)
            if 0 <= finishing < count:
                store(finishing)
            if i == 1:
                group_wkvb(nc.vector.tensor_copy, 0)
                quantise_wkvb()
            if 0 <= expanding < count:
                expand(expanding)
